import numpy as np
import ml_dtypes


def mxq(x, axis, fmt="e4m3"):
    dtype, down = {"e4m3": (ml_dtypes.float8_e4m3fn, 7), "e5m2": (ml_dtypes.float8_e5m2, 14)}[fmt]
    v = np.moveaxis(np.asarray(x, np.float32).astype(ml_dtypes.bfloat16).astype(np.float64), axis, -1)
    blocks = v.reshape(v.shape[:-1] + (-1, 32))
    amax = np.abs(blocks).max(-1, keepdims=True)
    byte = np.maximum(np.where(amax > 0, np.frexp(amax)[1] - 1 + 127, 0) - down, 1)
    scale = np.exp2(byte - 127.0)
    codes = (blocks / scale).astype(np.float32).astype(dtype).astype(np.float64)
    return np.moveaxis((codes * scale).reshape(v.shape), -1, axis)


WIDE = False


def mx_kscale(k):
    if not WIDE:
        return np.ones(k)
    levels = np.array([10, -10, 5, -5, 0])
    if k % 512:
        return np.exp2(np.random.permutation(np.resize(levels, k // 32))).repeat(32)
    a = np.empty((k // 512, 16))
    for p in range(k // 512):
        a[p, :8] = np.random.permutation(np.resize(levels, 8))
        for g in range(8):
            far = levels[np.abs(levels - a[p, g]) >= 10]
            a[p, g + 8] = far[np.random.randint(len(far))]
    return np.exp2(a.ravel()).repeat(32)


BF16 = ml_dtypes.bfloat16


def bf(x):
    return np.asarray(x, np.float32).astype(BF16)


def f64(x):
    return np.asarray(x).astype(np.float64)


B, T, D, H, DH, R, F = 1, 512, 1024, 4, 256, 64, 4096
EPS = 1e-5
E = H * DH


def rope(u, c, s):
    ur, up = u[..., :R], u[..., R:]
    c = c[None, :, None, :]
    s = s[None, :, None, :]
    ue, uo = ur[..., ::2], ur[..., 1::2]
    ur2 = np.stack([ue * c - uo * s, uo * c + ue * s], axis=-1).reshape(ur.shape)
    return np.concatenate([ur2, up], axis=-1)


def setup_inputs():
    rn = np.random.standard_normal
    s = mx_kscale(D)
    ang = np.random.uniform(0.0, 2.0 * np.pi, (T, R // 2))
    return {
        "x": bf(3.0 * np.sqrt(EPS) * (rn((B, T, D)) + 0.5 * rn((B, T, 1)))),
        "ln_scale": bf((1.0 + 0.1 * rn(D)) * s),
        "ln_offset": bf(0.1 * rn(D) * s),
        "wq": bf(rn((D, E)) / np.sqrt(D) / s[:, None]),
        "wk": bf(rn((D, E)) / np.sqrt(D) / s[:, None]),
        "wv": bf(rn((D, E)) / np.sqrt(D) / s[:, None]),
        "rope_cos": bf(np.cos(ang)),
        "rope_sin": bf(np.sin(ang)),
    }


def reference(x, ln_scale, ln_offset, wq, wk, wv, rope_cos, rope_sin):
    x = f64(x)
    mean = x.mean(-1, keepdims=True)
    var = ((x - mean) ** 2).mean(-1, keepdims=True)
    xn = (x - mean) * (1.0 / np.sqrt(var + EPS))
    xn = xn * f64(ln_scale) + f64(ln_offset)
    xq = mxq(xn, 2, "e4m3")
    q = (xq @ mxq(f64(wq), 0, "e4m3")).reshape(B, T, H, DH)
    k = (xq @ mxq(f64(wk), 0, "e4m3")).reshape(B, T, H, DH)
    v = (xq @ mxq(f64(wv), 0, "e4m3")).reshape(B, T, H, DH)
    c, s = f64(rope_cos), f64(rope_sin)
    return rope(q, c, s), rope(k, c, s), v

@@ -1,0 +1,241 @@
+from contextlib import ExitStack
+
+import concourse.mybir as mybir
+from concourse.masks import make_identity
+
+F32 = mybir.dt.float32
+BF16 = mybir.dt.bfloat16
+I32 = mybir.dt.int32
+U32 = mybir.dt.uint32
+U8 = mybir.dt.uint8
+FP8X4 = mybir.dt.float8_e4m3fn_x4
+ALU = mybir.AluOpType
+
+P = 128
+TOKENS = 512
+D_MODEL = 1024
+HEADS = 4
+HEAD_DIM = 256
+ROTATED = 64
+PAIRS = ROTATED // 2
+WIDTH = HEADS * HEAD_DIM
+EPS = 1e-5
+
+TOKEN_TILES = TOKENS // P
+PACK = 4
+K_PASS = P * PACK
+PASSES = D_MODEL // K_PASS
+BANK = 512
+PSUM_BANKS = 8
+STATS_WIDTH = 512
+STATS_DIM = 6
+HALF = WIDTH // 2
+EARLY_CHUNKS = 4
+
+FLOPS = 2 * TOKENS * D_MODEL * 3 * WIDTH
+
+
+def tile_transformerlayershard_pa_kernel(
+    tc, x, ln_scale, ln_offset, wq, wk, wv, rope_cos, rope_sin, out_0, out_1, out_2
+):
+    nc = tc.nc
+    weights = [wv, wq, wk]
+    outputs = [out_2, out_0, out_1]
+    rotated_projections = (1, 2)
+    chunks = len(weights) * PASSES
+
+    with ExitStack() as stack:
+        keep = stack.enter_context(tc.tile_pool(name="keep", bufs=1))
+        per_tile = stack.enter_context(tc.tile_pool(name="per_tile", bufs=TOKEN_TILES))
+        results = stack.enter_context(tc.tile_pool(name="results", bufs=2 * TOKEN_TILES))
+        banks = stack.enter_context(tc.psum_pool(name="banks", bufs=PSUM_BANKS))
+        stack.enter_context(tc.manual_schedule())
+
+        cos_bf = keep.tile([P, TOKEN_TILES, PAIRS], BF16)
+        sin_bf = keep.tile([P, TOKEN_TILES, PAIRS], BF16)
+        nc.scalar.dma_start(out=cos_bf[:], in_=rope_cos.rearrange("(p a) i -> p a i", a=TOKEN_TILES))
+        nc.scalar.dma_start(out=sin_bf[:], in_=rope_sin.rearrange("(p a) i -> p a i", a=TOKEN_TILES))
+
+        x_rows = x.flatten_outer_dims().rearrange("(p a) d -> p a d", a=TOKEN_TILES)
+        x_sb = keep.tile([P, TOKEN_TILES, D_MODEL], BF16)
+        for a in range(TOKEN_TILES):
+            nc.sync.dma_start(out=x_sb[:, a, :], in_=x_rows[:, a, :])
+
+        affine_rows = keep.tile([P, 2 * D_MODEL], BF16)
+        nc.vector.memset(affine_rows[:].bitcast(I32), 0)
+        nc.sync.dma_start(out=affine_rows[0:1, 0:D_MODEL], in_=ln_scale.rearrange("(o d) -> o d", o=1))
+        nc.sync.dma_start(out=affine_rows[0:1, D_MODEL : 2 * D_MODEL], in_=ln_offset.rearrange("(o d) -> o d", o=1))
+
+        w_raw = []
+        for c in range(chunks):
+            rows = weights[c // PASSES][(c % PASSES) * K_PASS : (c % PASSES + 1) * K_PASS, :]
+            w_raw.append(keep.tile([P, PACK, WIDTH], BF16, name="w_raw_%d" % c))
+            nc.sync.dma_start(
+                out=w_raw[c][:].rearrange("q t n -> q (t n)"),
+                in_=rows.rearrange("(q t) n -> q (t n)", t=PACK),
+            )
+
+        ones = keep.tile([P, P], BF16)
+        nc.vector.memset(ones[:], 1.0)
+        warm = keep.tile([P, 1], F32)
+        nc.vector.memset(warm[:], 1.0)
+        nc.scalar.sqrt(warm[:], warm[:])
+        identity = keep.tile([P, P], F32)
+        make_identity(nc, identity[:])
+
+        cos_twice = keep.tile([P, TOKEN_TILES, PAIRS, 2], F32)
+        nc.gpsimd.tensor_copy(out=cos_twice[:], in_=cos_bf[:].unsqueeze(3).to_broadcast([P, TOKEN_TILES, PAIRS, 2]))
+        signed_sin = keep.tile([P, TOKEN_TILES, 2, PAIRS], F32)
+        nc.gpsimd.tensor_scalar(
+            out=signed_sin[:, :, 0, :], in0=sin_bf[:], scalar1=-1.0, scalar2=0.0, op0=ALU.mult, op1=ALU.add
+        )
+        nc.gpsimd.tensor_copy(out=signed_sin[:, :, 1, :], in_=sin_bf[:])
+
+        affine_banks = []
+        for first in range(0, 2 * D_MODEL, BANK):
+            affine_banks.append(banks.tile([P, BANK], F32, name="affine_%d" % first, tag="bank"))
+            nc.tensor.matmul(
+                out=affine_banks[-1][:], lhsT=ones[:], rhs=affine_rows[:, first : first + BANK], start=True, stop=True
+            )
+        gain_banks = affine_banks[0 : D_MODEL // BANK]
+        offset_banks = affine_banks[D_MODEL // BANK :]
+
+        w_codes = keep.tile([P, chunks, WIDTH], U32, align_bytes=64)
+        w_scales = keep.tile([P, chunks, WIDTH], U8, align_bytes=64)
+        grouped = []
+        for c in range(chunks):
+            grouped.append(keep.tile([P, WIDTH, PACK], BF16, name="grouped_%d" % c, align_bytes=64))
+
+        def regroup_views(c, half, run):
+            cols = slice(half * HALF, (half + 1) * HALF)
+            dst = grouped[c][:, cols, :].rearrange("q (n i) t -> q n t i", i=run)
+            src = w_raw[c][:, :, cols].rearrange("q t (n i) -> q n t i", i=run)
+            return dst, src
+
+        def regroup_on_scalar(c):
+            dst, src = regroup_views(c, 0, 4)
+            nc.scalar.copy(out=dst, in_=src)
+
+        def regroup_on_vector(c):
+            dst, src = regroup_views(c, 1, 4)
+            nc.vector.tensor_copy(out=dst, in_=src)
+
+        def regroup_on_gpsimd(c):
+            dst, src = regroup_views(c, 1, 1)
+            nc.gpsimd.tensor_scalar(out=dst, in0=src, scalar1=1.0, scalar2=0.0, op0=ALU.mult, op1=ALU.add)
+
+        def quantise_weights(c):
+            nc.vector.quantize_mx(
+                out=w_codes[:, c, :].bitcast(FP8X4), scales=w_scales[:, c, :],
+                in_=grouped[c][:].rearrange("q n t -> q (n t)"),
+            )
+
+        regroup_on_scalar(0)
+        regroup_on_gpsimd(0)
+
+        stats = keep.tile([P, TOKEN_TILES, D_MODEL // STATS_WIDTH, STATS_DIM], F32)
+        mean_var = keep.tile([P, TOKEN_TILES, 2], F32)
+        for a in range(TOKEN_TILES):
+            for s in range(D_MODEL // STATS_WIDTH):
+                nc.vector.bn_stats(out=stats[:, a, s, :], in_=x_sb[:, a, s * STATS_WIDTH : (s + 1) * STATS_WIDTH])
+        for a in range(TOKEN_TILES):
+            nc.vector.bn_aggr(out=mean_var[:, a, :], in_=stats[:, a, :, :].rearrange("p s v -> p (s v)"))
+        rstd = keep.tile([P, TOKEN_TILES], F32)
+        nc.vector.tensor_scalar(out=rstd[:], in0=mean_var[:, :, 1], scalar1=EPS, scalar2=None, op0=ALU.add)
+        nc.scalar.sqrt(rstd[:], rstd[:])
+
+        centred = []
+        for a in range(TOKEN_TILES):
+            centred.append(per_tile.tile([P, D_MODEL], F32, name="centred"))
+            for h, first in enumerate(range(0, D_MODEL, BANK)):
+                cols = slice(first, first + BANK)
+                nc.vector.scalar_tensor_tensor(
+                    out=centred[a][:, cols], in0=x_sb[:, a, cols], scalar=mean_var[:, a, 0:1],
+                    in1=gain_banks[h][:], op0=ALU.subtract, op1=ALU.mult,
+                )
+        nc.vector.reciprocal(rstd[:], rstd[:])
+
+        for c in range(1, EARLY_CHUNKS):
+            regroup_on_scalar(c)
+            regroup_on_gpsimd(c)
+
+        x_grouped = []
+        for a in range(TOKEN_TILES):
+            xn = per_tile.tile([P, D_MODEL], BF16)
+            for h, first in enumerate(range(0, D_MODEL, BANK)):
+                cols = slice(first, first + BANK)
+                nc.vector.scalar_tensor_tensor(
+                    out=xn[:, cols], in0=centred[a][:, cols], scalar=rstd[:, a : a + 1],
+                    in1=offset_banks[h][:], op0=ALU.mult, op1=ALU.add,
+                )
+            xn_words = xn[:].bitcast(F32)
+            xt = banks.tile([P, PASSES * 2, P], F32, tag="bank")
+            for b in range(PASSES * 2):
+                nc.tensor.transpose(out=xt[:, b, :], in_=xn_words[:, (b // 2) * 2 * P + b % 2 : (b // 2 + 1) * 2 * P : 2], identity=identity[:])
+            x_grouped.append(per_tile.tile([P, PASSES * P * PACK], BF16, name="x_grouped", align_bytes=64))
+            nc.scalar.copy(
+                out=x_grouped[a][:].bitcast(F32).rearrange("q (g r u) -> q g r u", g=PASSES, u=2),
+                in_=xt[:].rearrange("q (g u) r -> q g r u", u=2),
+            )
+
+        x_codes = keep.tile([P, TOKEN_TILES, PASSES * P], U32, align_bytes=64)
+        x_scales = keep.tile([P, TOKEN_TILES, PASSES * P], U8, align_bytes=64)
+        quantise_weights(0)
+        quantise_weights(1)
+        for a in range(TOKEN_TILES):
+            nc.vector.quantize_mx(out=x_codes[:, a, :].bitcast(FP8X4), scales=x_scales[:, a, :], in_=x_grouped[a][:])
+        for c in range(EARLY_CHUNKS, chunks):
+            regroup_on_scalar(c)
+            regroup_on_vector(c)
+            quantise_weights(c - 2)
+        for c in range(chunks - 2, chunks):
+            quantise_weights(c)
+
+        result = {}
+        for m in range(len(weights)):
+            out_rows = outputs[m].flatten_outer_dims().rearrange("(p a h) d -> p a (h d)", a=TOKEN_TILES, h=HEADS)
+            for a in range(TOKEN_TILES):
+                result[m, a] = results.tile([P, WIDTH], F32, name="result")
+                for first in range(0, WIDTH, BANK):
+                    bank = banks.tile([P, BANK], F32, tag="bank")
+                    for g in range(PASSES):
+                        nc.tensor.matmul_mx(
+                            out=bank[:],
+                            lhsT=x_codes[:, a, g * P : (g + 1) * P].bitcast(FP8X4),
+                            lhsT_scale=x_scales[:, a, g * P : (g + 1) * P],
+                            rhs=w_codes[:, m * PASSES + g, first : first + BANK].bitcast(FP8X4),
+                            rhs_scale=w_scales[:, m * PASSES + g, first : first + BANK],
+                            start=(g == 0),
+                            stop=(g == PASSES - 1),
+                        )
+                    nc.scalar.copy(out=result[m, a][:, first : first + BANK], in_=bank[:])
+                if m not in rotated_projections:
+                    nc.sync.dma_start(out=out_rows[:, a, :], in_=result[m, a][:])
+
+        to_rotate = [(m, a) for m in rotated_projections for a in range(TOKEN_TILES)]
+        cross = {}
+        for j in range(len(to_rotate) + 1):
+            if j < len(to_rotate):
+                m, a = to_rotate[j]
+                u = result[m, a][:].rearrange("p (h d) -> p h d", h=HEADS)[:, :, 0:ROTATED]
+                u_pairs = u.rearrange("p h (i e) -> p h i e", e=2)
+                cross[m, a] = per_tile.tile([P, 2, HEADS, PAIRS], F32, name="cross")
+                for e in range(2):
+                    nc.vector.tensor_tensor(
+                        out=cross[m, a][:, e, :, :], in0=u_pairs[:, :, :, 1 - e],
+                        in1=signed_sin[:, a, e, :].unsqueeze(1).to_broadcast([P, HEADS, PAIRS]), op=ALU.mult,
+                    )
+                nc.vector.tensor_tensor(
+                    out=u, in0=u,
+                    in1=cos_twice[:, a, :, :].rearrange("p i e -> p (i e)").unsqueeze(1).to_broadcast([P, HEADS, ROTATED]),
+                    op=ALU.mult,
+                )
+            if j > 0:
+                m, a = to_rotate[j - 1]
+                u = result[m, a][:].rearrange("p (h d) -> p h d", h=HEADS)[:, :, 0:ROTATED]
+                u_pairs = u.rearrange("p h (i e) -> p h i e", e=2)
+                nc.vector.tensor_tensor(
+                    out=u_pairs, in0=u_pairs, in1=cross[m, a][:].rearrange("p e h i -> p h i e"), op=ALU.add
+                )
+                out_rows = outputs[m].flatten_outer_dims().rearrange("(p a h) d -> p a (h d)", a=TOKEN_TILES, h=HEADS)
+                nc.sync.dma_start(out=out_rows[:, a, :], in_=result[m, a][:])

@@ -41,13 +41,13 @@ def tile_transformerlayershard_pa_kernel(
     nc = tc.nc
     weights = [wv, wq, wk]
     outputs = [out_2, out_0, out_1]
-    rotated_projections = (1, 2)
     chunks = len(weights) * PASSES
 
     with ExitStack() as stack:
         keep = stack.enter_context(tc.tile_pool(name="keep", bufs=1))
         per_tile = stack.enter_context(tc.tile_pool(name="per_tile", bufs=TOKEN_TILES))
-        results = stack.enter_context(tc.tile_pool(name="results", bufs=2 * TOKEN_TILES))
+        singles = stack.enter_context(tc.tile_pool(name="singles", bufs=TOKEN_TILES))
+        doubles = stack.enter_context(tc.tile_pool(name="doubles", bufs=3))
         banks = stack.enter_context(tc.psum_pool(name="banks", bufs=PSUM_BANKS))
         stack.enter_context(tc.manual_schedule())
 
@@ -56,24 +56,29 @@ def tile_transformerlayershard_pa_kernel(
         nc.scalar.dma_start(out=cos_bf[:], in_=rope_cos.rearrange("(p a) i -> p a i", a=TOKEN_TILES))
         nc.scalar.dma_start(out=sin_bf[:], in_=rope_sin.rearrange("(p a) i -> p a i", a=TOKEN_TILES))
 
+        affine_rows = keep.tile([P, 2 * D_MODEL], BF16)
+        nc.vector.memset(affine_rows[:].bitcast(I32), 0)
+
+        w_raw = {}
+
+        def load_weights(c, first, width):
+            rows = weights[c // PASSES][(c % PASSES) * K_PASS : (c % PASSES + 1) * K_PASS, first : first + width]
+            raw = keep.tile([P, PACK, width], BF16, name="w_raw_%d_%d" % (c, first))
+            nc.sync.dma_start(out=raw[:], in_=rows.rearrange("(q t) n -> q t n", t=PACK))
+            for half in range(first // HALF, (first + width) // HALF):
+                w_raw[c, half] = raw[:, :, half * HALF - first : (half + 1) * HALF - first]
+
         x_rows = x.flatten_outer_dims().rearrange("(p a) d -> p a d", a=TOKEN_TILES)
         x_sb = keep.tile([P, TOKEN_TILES, D_MODEL], BF16)
         for a in range(TOKEN_TILES):
             nc.sync.dma_start(out=x_sb[:, a, :], in_=x_rows[:, a, :])
-
-        affine_rows = keep.tile([P, 2 * D_MODEL], BF16)
-        nc.vector.memset(affine_rows[:].bitcast(I32), 0)
-        nc.sync.dma_start(out=affine_rows[0:1, 0:D_MODEL], in_=ln_scale.rearrange("(o d) -> o d", o=1))
-        nc.sync.dma_start(out=affine_rows[0:1, D_MODEL : 2 * D_MODEL], in_=ln_offset.rearrange("(o d) -> o d", o=1))
-
-        w_raw = []
-        for c in range(chunks):
-            rows = weights[c // PASSES][(c % PASSES) * K_PASS : (c % PASSES + 1) * K_PASS, :]
-            w_raw.append(keep.tile([P, PACK, WIDTH], BF16, name="w_raw_%d" % c))
-            nc.sync.dma_start(
-                out=w_raw[c][:].rearrange("q t n -> q (t n)"),
-                in_=rows.rearrange("(q t) n -> q (t n)", t=PACK),
-            )
+            if a % 2 == 1:
+                load_weights(0, (a // 2) * HALF, HALF)
+            if a == 1:
+                nc.sync.dma_start(out=affine_rows[0:1, 0:D_MODEL], in_=ln_scale.rearrange("(o d) -> o d", o=1))
+                nc.sync.dma_start(out=affine_rows[0:1, D_MODEL : 2 * D_MODEL], in_=ln_offset.rearrange("(o d) -> o d", o=1))
+        for c in range(1, chunks):
+            load_weights(c, 0, WIDTH)
 
         ones = keep.tile([P, P], BF16)
         nc.vector.memset(ones[:], 1.0)
@@ -85,11 +90,11 @@ def tile_transformerlayershard_pa_kernel(
 
         cos_twice = keep.tile([P, TOKEN_TILES, PAIRS, 2], F32)
         nc.gpsimd.tensor_copy(out=cos_twice[:], in_=cos_bf[:].unsqueeze(3).to_broadcast([P, TOKEN_TILES, PAIRS, 2]))
-        signed_sin = keep.tile([P, TOKEN_TILES, 2, PAIRS], F32)
+        signed_sin = keep.tile([P, TOKEN_TILES, PAIRS, 2], F32)
         nc.gpsimd.tensor_scalar(
-            out=signed_sin[:, :, 0, :], in0=sin_bf[:], scalar1=-1.0, scalar2=0.0, op0=ALU.mult, op1=ALU.add
+            out=signed_sin[:, :, :, 0], in0=sin_bf[:], scalar1=-1.0, scalar2=0.0, op0=ALU.mult, op1=ALU.add
         )
-        nc.gpsimd.tensor_copy(out=signed_sin[:, :, 1, :], in_=sin_bf[:])
+        nc.gpsimd.tensor_copy(out=signed_sin[:, :, :, 1], in_=sin_bf[:])
 
         affine_banks = []
         for first in range(0, 2 * D_MODEL, BANK):
@@ -109,7 +114,7 @@ def tile_transformerlayershard_pa_kernel(
         def regroup_views(c, half, run):
             cols = slice(half * HALF, (half + 1) * HALF)
             dst = grouped[c][:, cols, :].rearrange("q (n i) t -> q n t i", i=run)
-            src = w_raw[c][:, :, cols].rearrange("q t (n i) -> q n t i", i=run)
+            src = w_raw[c, half].rearrange("q t (n i) -> q n t i", i=run)
             return dst, src
 
         def regroup_on_scalar(c):
@@ -160,6 +165,7 @@ def tile_transformerlayershard_pa_kernel(
             regroup_on_gpsimd(c)
 
         x_grouped = []
+        x_banks = []
         for a in range(TOKEN_TILES):
             xn = per_tile.tile([P, D_MODEL], BF16)
             for h, first in enumerate(range(0, D_MODEL, BANK)):
@@ -172,11 +178,17 @@ def tile_transformerlayershard_pa_kernel(
             xt = banks.tile([P, PASSES * 2, P], F32, tag="bank")
             for b in range(PASSES * 2):
                 nc.tensor.transpose(out=xt[:, b, :], in_=xn_words[:, (b // 2) * 2 * P + b % 2 : (b // 2 + 1) * 2 * P : 2], identity=identity[:])
+            x_banks.append(xt)
+
+        for a in range(TOKEN_TILES):
             x_grouped.append(per_tile.tile([P, PASSES * P * PACK], BF16, name="x_grouped", align_bytes=64))
             nc.scalar.copy(
                 out=x_grouped[a][:].bitcast(F32).rearrange("q (g r u) -> q g r u", g=PASSES, u=2),
-                in_=xt[:].rearrange("q (g u) r -> q g r u", u=2),
+                in_=x_banks[a][:].rearrange("q (g u) r -> q g r u", u=2),
             )
+            if a == 0:
+                regroup_on_scalar(EARLY_CHUNKS)
+        regroup_on_scalar(EARLY_CHUNKS + 1)
 
         x_codes = keep.tile([P, TOKEN_TILES, PASSES * P], U32, align_bytes=64)
         x_scales = keep.tile([P, TOKEN_TILES, PASSES * P], U8, align_bytes=64)
@@ -185,17 +197,12 @@ def tile_transformerlayershard_pa_kernel(
         for a in range(TOKEN_TILES):
             nc.vector.quantize_mx(out=x_codes[:, a, :].bitcast(FP8X4), scales=x_scales[:, a, :], in_=x_grouped[a][:])
         for c in range(EARLY_CHUNKS, chunks):
-            regroup_on_scalar(c)
             regroup_on_vector(c)
             quantise_weights(c - 2)
-        for c in range(chunks - 2, chunks):
-            quantise_weights(c)
 
-        result = {}
-        for m in range(len(weights)):
-            out_rows = outputs[m].flatten_outer_dims().rearrange("(p a h) d -> p a (h d)", a=TOKEN_TILES, h=HEADS)
-            for a in range(TOKEN_TILES):
-                result[m, a] = results.tile([P, WIDTH], F32, name="result")
+        def project(m, group):
+            result = (singles if len(group) == 1 else doubles).tile([P, len(group), WIDTH], F32, name="result")
+            for i, a in enumerate(group):
                 for first in range(0, WIDTH, BANK):
                     bank = banks.tile([P, BANK], F32, tag="bank")
                     for g in range(PASSES):
@@ -208,34 +215,44 @@ def tile_transformerlayershard_pa_kernel(
                             start=(g == 0),
                             stop=(g == PASSES - 1),
                         )
-                    nc.scalar.copy(out=result[m, a][:, first : first + BANK], in_=bank[:])
-                if m not in rotated_projections:
-                    nc.sync.dma_start(out=out_rows[:, a, :], in_=result[m, a][:])
+                    nc.scalar.copy(out=result[:, i, first : first + BANK], in_=bank[:])
+            return result
 
-        to_rotate = [(m, a) for m in rotated_projections for a in range(TOKEN_TILES)]
-        cross = {}
-        for j in range(len(to_rotate) + 1):
-            if j < len(to_rotate):
-                m, a = to_rotate[j]
-                u = result[m, a][:].rearrange("p (h d) -> p h d", h=HEADS)[:, :, 0:ROTATED]
-                u_pairs = u.rearrange("p h (i e) -> p h i e", e=2)
-                cross[m, a] = per_tile.tile([P, 2, HEADS, PAIRS], F32, name="cross")
-                for e in range(2):
-                    nc.vector.tensor_tensor(
-                        out=cross[m, a][:, e, :, :], in0=u_pairs[:, :, :, 1 - e],
-                        in1=signed_sin[:, a, e, :].unsqueeze(1).to_broadcast([P, HEADS, PAIRS]), op=ALU.mult,
-                    )
-                nc.vector.tensor_tensor(
-                    out=u, in0=u,
-                    in1=cos_twice[:, a, :, :].rearrange("p i e -> p (i e)").unsqueeze(1).to_broadcast([P, HEADS, ROTATED]),
-                    op=ALU.mult,
-                )
-            if j > 0:
-                m, a = to_rotate[j - 1]
-                u = result[m, a][:].rearrange("p (h d) -> p h d", h=HEADS)[:, :, 0:ROTATED]
-                u_pairs = u.rearrange("p h (i e) -> p h i e", e=2)
-                nc.vector.tensor_tensor(
-                    out=u_pairs, in0=u_pairs, in1=cross[m, a][:].rearrange("p e h i -> p h i e"), op=ALU.add
-                )
-                out_rows = outputs[m].flatten_outer_dims().rearrange("(p a h) d -> p a (h d)", a=TOKEN_TILES, h=HEADS)
-                nc.sync.dma_start(out=out_rows[:, a, :], in_=result[m, a][:])
+        def store(m, group, result):
+            out_rows = outputs[m].flatten_outer_dims().rearrange("(p a h) d -> p a (h d)", a=TOKEN_TILES, h=HEADS)
+            nc.sync.dma_start(out=out_rows[:, group[0] : group[-1] + 1, :], in_=result[:])
+
+        def rotate(group, result):
+            u = result[:].rearrange("p a (h d) -> p a h d", h=HEADS)[:, :, :, 0:ROTATED]
+            swapped = u.rearrange("p a h (i e) -> p a h i e", e=2)[:, :, :, :, ::-1]
+            tiles = slice(group[0], group[-1] + 1)
+            cross = doubles.tile([P, len(group), HEADS, PAIRS, 2], F32, name="cross")
+            nc.vector.tensor_tensor(
+                out=cross[:], in0=swapped,
+                in1=signed_sin[:, tiles, :, :].unsqueeze(2).to_broadcast([P, len(group), HEADS, PAIRS, 2]), op=ALU.mult,
+            )
+            nc.vector.tensor_tensor(
+                out=u, in0=u,
+                in1=cos_twice[:, tiles, :, :].rearrange("p a i e -> p a (i e)").unsqueeze(2).to_broadcast(
+                    [P, len(group), HEADS, ROTATED]
+                ),
+                op=ALU.mult,
+            )
+            nc.vector.tensor_tensor(out=u, in0=u, in1=cross[:].rearrange("p a h i e -> p a h (i e)"), op=ALU.add)
+
+        for a in range(TOKEN_TILES):
+            store(0, [a], project(0, [a]))
+        quantise_weights(chunks - 2)
+        rotated_groups = [(1, [0, 1]), (1, [2, 3]), (2, [0, 1]), (2, [2]), (2, [3])]
+        waiting = []
+        for m, group in rotated_groups:
+            waiting.append((m, group, project(m, group)))
+            if len(waiting) == 1:
+                quantise_weights(chunks - 1)
+            else:
+                m_done, group_done, result = waiting[-2]
+                rotate(group_done, result)
+                store(m_done, group_done, result)
+        m_done, group_done, result = waiting[-1]
+        rotate(group_done, result)
+        store(m_done, group_done, result)

@@ -30,6 +30,7 @@ PSUM_BANKS = 8
 STATS_WIDTH = 512
 STATS_DIM = 6
 HALF = WIDTH // 2
+HALF_HEAD = HEAD_DIM // 2
 EARLY_CHUNKS = 4
 
 FLOPS = 2 * TOKENS * D_MODEL * 3 * WIDTH
@@ -46,10 +47,13 @@ def tile_transformerlayershard_pa_kernel(
     with ExitStack() as stack:
         keep = stack.enter_context(tc.tile_pool(name="keep", bufs=1))
         per_tile = stack.enter_context(tc.tile_pool(name="per_tile", bufs=TOKEN_TILES))
-        singles = stack.enter_context(tc.tile_pool(name="singles", bufs=TOKEN_TILES))
-        doubles = stack.enter_context(tc.tile_pool(name="doubles", bufs=3))
-        banks = stack.enter_context(tc.psum_pool(name="banks", bufs=PSUM_BANKS))
+        halves = stack.enter_context(tc.tile_pool(name="halves", bufs=2 * TOKEN_TILES))
+        results = stack.enter_context(tc.tile_pool(name="results", bufs=2 * TOKEN_TILES))
+        banks = stack.enter_context(tc.psum_pool(name="banks", bufs=1))
         stack.enter_context(tc.manual_schedule())
+
+        def in_bank(number, shape, dtype, name):
+            return banks.tile(shape, dtype, name=name, tag="bank_%d" % number)
 
         cos_bf = keep.tile([P, TOKEN_TILES, PAIRS], BF16)
         sin_bf = keep.tile([P, TOKEN_TILES, PAIRS], BF16)
@@ -60,11 +64,13 @@ def tile_transformerlayershard_pa_kernel(
         nc.vector.memset(affine_rows[:].bitcast(I32), 0)
 
         w_raw = {}
+        w_whole = {}
 
         def load_weights(c, first, width):
             rows = weights[c // PASSES][(c % PASSES) * K_PASS : (c % PASSES + 1) * K_PASS, first : first + width]
             raw = keep.tile([P, PACK, width], BF16, name="w_raw_%d_%d" % (c, first))
             nc.sync.dma_start(out=raw[:], in_=rows.rearrange("(q t) n -> q t n", t=PACK))
+            w_whole[c] = raw[:]
             for half in range(first // HALF, (first + width) // HALF):
                 w_raw[c, half] = raw[:, :, half * HALF - first : (half + 1) * HALF - first]
 
@@ -98,7 +104,7 @@ def tile_transformerlayershard_pa_kernel(
 
         affine_banks = []
         for first in range(0, 2 * D_MODEL, BANK):
-            affine_banks.append(banks.tile([P, BANK], F32, name="affine_%d" % first, tag="bank"))
+            affine_banks.append(in_bank(first // BANK, [P, BANK], F32, "affine_%d" % first))
             nc.tensor.matmul(
                 out=affine_banks[-1][:], lhsT=ones[:], rhs=affine_rows[:, first : first + BANK], start=True, stop=True
             )
@@ -111,23 +117,37 @@ def tile_transformerlayershard_pa_kernel(
         for c in range(chunks):
             grouped.append(keep.tile([P, WIDTH, PACK], BF16, name="grouped_%d" % c, align_bytes=64))
 
-        def regroup_views(c, half, run):
-            cols = slice(half * HALF, (half + 1) * HALF)
-            dst = grouped[c][:, cols, :].rearrange("q (n i) t -> q n t i", i=run)
-            src = w_raw[c, half].rearrange("q t (n i) -> q n t i", i=run)
-            return dst, src
+        def regroup_views(c, half, run, part=0, parts=1):
+            width = HALF // parts
+            dst = grouped[c][:, half * HALF + part * width : half * HALF + (part + 1) * width, :]
+            if c < PASSES:
+                src = w_raw[c, half][:, :, part * width : (part + 1) * width]
+                return dst.rearrange("q (n i) t -> q n t i", i=run), src.rearrange("q t (n i) -> q n t i", i=run)
+            heads = HEADS // parts
+            src = w_whole[c].rearrange("q t (h s d) -> q t s h d", s=2, d=HALF_HEAD)[:, :, half, :, :]
+            return (
+                dst.rearrange("q (h n i) t -> q h n t i", h=heads, i=run),
+                src[:, :, part * heads : (part + 1) * heads, :].rearrange("q t h (n i) -> q h n t i", i=run),
+            )
 
-        def regroup_on_scalar(c):
-            dst, src = regroup_views(c, 0, 4)
+        def regroup_on_scalar(c, half, part=0, parts=1):
+            dst, src = regroup_views(c, half, 4, part, parts)
             nc.scalar.copy(out=dst, in_=src)
 
-        def regroup_on_vector(c):
-            dst, src = regroup_views(c, 1, 4)
+        def regroup_on_vector(c, half):
+            dst, src = regroup_views(c, half, 4)
             nc.vector.tensor_copy(out=dst, in_=src)
 
-        def regroup_on_gpsimd(c):
-            dst, src = regroup_views(c, 1, 1)
+        def regroup_on_gpsimd(c, half):
+            dst, src = regroup_views(c, half, 1)
             nc.gpsimd.tensor_scalar(out=dst, in0=src, scalar1=1.0, scalar2=0.0, op0=ALU.mult, op1=ALU.add)
+
+        def quantise_half(c, half):
+            cols = slice(half * HALF, (half + 1) * HALF)
+            nc.vector.quantize_mx(
+                out=w_codes[:, c, cols].bitcast(FP8X4), scales=w_scales[:, c, cols],
+                in_=grouped[c][:, cols, :].rearrange("q n t -> q (n t)"),
+            )
 
         def quantise_weights(c):
             nc.vector.quantize_mx(
@@ -135,8 +155,8 @@ def tile_transformerlayershard_pa_kernel(
                 in_=grouped[c][:].rearrange("q n t -> q (n t)"),
             )
 
-        regroup_on_scalar(0)
-        regroup_on_gpsimd(0)
+        regroup_on_scalar(0, 0)
+        regroup_on_gpsimd(0, 1)
 
         stats = keep.tile([P, TOKEN_TILES, D_MODEL // STATS_WIDTH, STATS_DIM], F32)
         mean_var = keep.tile([P, TOKEN_TILES, 2], F32)
@@ -160,13 +180,11 @@ def tile_transformerlayershard_pa_kernel(
                 )
         nc.vector.reciprocal(rstd[:], rstd[:])
 
-        for c in range(1, EARLY_CHUNKS):
-            regroup_on_scalar(c)
-            regroup_on_gpsimd(c)
+        x_grouped = {}
+        x_codes = keep.tile([P, TOKEN_TILES, PASSES * P], U32, align_bytes=64)
+        x_scales = keep.tile([P, TOKEN_TILES, PASSES * P], U8, align_bytes=64)
 
-        x_grouped = []
-        x_banks = []
-        for a in range(TOKEN_TILES):
+        def normalise(a, number):
             xn = per_tile.tile([P, D_MODEL], BF16)
             for h, first in enumerate(range(0, D_MODEL, BANK)):
                 cols = slice(first, first + BANK)
@@ -175,84 +193,106 @@ def tile_transformerlayershard_pa_kernel(
                     in1=offset_banks[h][:], op0=ALU.mult, op1=ALU.add,
                 )
             xn_words = xn[:].bitcast(F32)
-            xt = banks.tile([P, PASSES * 2, P], F32, tag="bank")
+            xt = in_bank(number, [P, PASSES * 2, P], F32, "xt")
             for b in range(PASSES * 2):
-                nc.tensor.transpose(out=xt[:, b, :], in_=xn_words[:, (b // 2) * 2 * P + b % 2 : (b // 2 + 1) * 2 * P : 2], identity=identity[:])
-            x_banks.append(xt)
-
-        for a in range(TOKEN_TILES):
-            x_grouped.append(per_tile.tile([P, PASSES * P * PACK], BF16, name="x_grouped", align_bytes=64))
+                nc.tensor.transpose(
+                    out=xt[:, b, :], in_=xn_words[:, (b // 2) * 2 * P + b % 2 : (b // 2 + 1) * 2 * P : 2], identity=identity[:]
+                )
+            x_grouped[a] = per_tile.tile([P, PASSES * P * PACK], BF16, name="x_grouped", align_bytes=64)
             nc.scalar.copy(
                 out=x_grouped[a][:].bitcast(F32).rearrange("q (g r u) -> q g r u", g=PASSES, u=2),
-                in_=x_banks[a][:].rearrange("q (g u) r -> q g r u", u=2),
+                in_=xt[:].rearrange("q (g u) r -> q g r u", u=2),
             )
-            if a == 0:
-                regroup_on_scalar(EARLY_CHUNKS)
-        regroup_on_scalar(EARLY_CHUNKS + 1)
 
-        x_codes = keep.tile([P, TOKEN_TILES, PASSES * P], U32, align_bytes=64)
-        x_scales = keep.tile([P, TOKEN_TILES, PASSES * P], U8, align_bytes=64)
-        quantise_weights(0)
-        quantise_weights(1)
-        for a in range(TOKEN_TILES):
+        def quantise_x(a):
             nc.vector.quantize_mx(out=x_codes[:, a, :].bitcast(FP8X4), scales=x_scales[:, a, :], in_=x_grouped[a][:])
-        for c in range(EARLY_CHUNKS, chunks):
-            regroup_on_vector(c)
-            quantise_weights(c - 2)
 
-        def project(m, group):
-            result = (singles if len(group) == 1 else doubles).tile([P, len(group), WIDTH], F32, name="result")
-            for i, a in enumerate(group):
-                for first in range(0, WIDTH, BANK):
-                    bank = banks.tile([P, BANK], F32, tag="bank")
-                    for g in range(PASSES):
-                        nc.tensor.matmul_mx(
-                            out=bank[:],
-                            lhsT=x_codes[:, a, g * P : (g + 1) * P].bitcast(FP8X4),
-                            lhsT_scale=x_scales[:, a, g * P : (g + 1) * P],
-                            rhs=w_codes[:, m * PASSES + g, first : first + BANK].bitcast(FP8X4),
-                            rhs_scale=w_scales[:, m * PASSES + g, first : first + BANK],
-                            start=(g == 0),
-                            stop=(g == PASSES - 1),
-                        )
-                    nc.scalar.copy(out=result[:, i, first : first + BANK], in_=bank[:])
-            return result
+        bank_order = [4, 5, 6, 7, 0, 1, 2, 3]
+        taken = []
 
-        def store(m, group, result):
-            out_rows = outputs[m].flatten_outer_dims().rearrange("(p a h) d -> p a (h d)", a=TOKEN_TILES, h=HEADS)
-            nc.sync.dma_start(out=out_rows[:, group[0] : group[-1] + 1, :], in_=result[:])
+        def multiply(m, a, first):
+            bank = in_bank(bank_order[len(taken) % PSUM_BANKS], [P, BANK], F32, "product")
+            taken.append(bank)
+            for g in range(PASSES):
+                nc.tensor.matmul_mx(
+                    out=bank[:],
+                    lhsT=x_codes[:, a, g * P : (g + 1) * P].bitcast(FP8X4),
+                    lhsT_scale=x_scales[:, a, g * P : (g + 1) * P],
+                    rhs=w_codes[:, m * PASSES + g, first : first + BANK].bitcast(FP8X4),
+                    rhs_scale=w_scales[:, m * PASSES + g, first : first + BANK],
+                    start=(g == 0),
+                    stop=(g == PASSES - 1),
+                )
+            return bank
 
-        def rotate(group, result):
-            u = result[:].rearrange("p a (h d) -> p a h d", h=HEADS)[:, :, :, 0:ROTATED]
-            swapped = u.rearrange("p a h (i e) -> p a h i e", e=2)[:, :, :, :, ::-1]
-            tiles = slice(group[0], group[-1] + 1)
-            cross = doubles.tile([P, len(group), HEADS, PAIRS, 2], F32, name="cross")
+        def output_rows(m, a):
+            return outputs[m].flatten_outer_dims().rearrange("(p a h) d -> p a (h d)", a=TOKEN_TILES, h=HEADS)[:, a, :]
+
+        def project_v(a, half):
+            cols = slice(half * HALF, (half + 1) * HALF)
+            result = halves.tile([P, HALF], F32, name="value")
+            nc.scalar.copy(out=result[:], in_=multiply(0, a, half * HALF)[:])
+            nc.sync.dma_start(out=output_rows(0, a)[:, cols], in_=result[:])
+
+        def project_rotated(m, a, last=False):
+            result = results.tile([P, WIDTH], F32, name="result")
+            u = multiply(m, a, 0)[:].rearrange("p (h d) -> p h d", d=HALF_HEAD)
+            rest = multiply(m, a, BANK)
+            r = result[:].rearrange("p (h d) -> p h d", d=HEAD_DIM)
+            cross = per_tile.tile([P, HEADS, PAIRS, 2], F32, name="cross")
             nc.vector.tensor_tensor(
-                out=cross[:], in0=swapped,
-                in1=signed_sin[:, tiles, :, :].unsqueeze(2).to_broadcast([P, len(group), HEADS, PAIRS, 2]), op=ALU.mult,
+                out=cross[:], in0=u[:, :, 0:ROTATED].rearrange("p h (i e) -> p h i e", e=2)[:, :, :, ::-1],
+                in1=signed_sin[:, a, :, :].unsqueeze(1).to_broadcast([P, HEADS, PAIRS, 2]), op=ALU.mult,
             )
             nc.vector.tensor_tensor(
-                out=u, in0=u,
-                in1=cos_twice[:, tiles, :, :].rearrange("p a i e -> p a (i e)").unsqueeze(2).to_broadcast(
-                    [P, len(group), HEADS, ROTATED]
-                ),
+                out=r[:, :, 0:ROTATED], in0=u[:, :, 0:ROTATED],
+                in1=cos_twice[:, a, :, :].rearrange("p i e -> p (i e)").unsqueeze(1).to_broadcast([P, HEADS, ROTATED]),
                 op=ALU.mult,
             )
-            nc.vector.tensor_tensor(out=u, in0=u, in1=cross[:].rearrange("p a h i e -> p a h (i e)"), op=ALU.add)
+            nc.scalar.copy(out=r[:, :, HALF_HEAD:], in_=rest[:].rearrange("p (h d) -> p h d", d=HALF_HEAD))
+            nc.scalar.copy(out=r[:, :, ROTATED:HALF_HEAD], in_=u[:, :, ROTATED:])
+            adder = nc.vector if last else nc.gpsimd
+            adder.tensor_tensor(
+                out=r[:, :, 0:ROTATED], in0=r[:, :, 0:ROTATED], in1=cross[:].rearrange("p h i e -> p h (i e)"), op=ALU.add
+            )
+            nc.sync.dma_start(out=output_rows(m, a), in_=result[:])
 
+        regroup_on_scalar(1, 0)
+        regroup_on_gpsimd(1, 1)
+        regroup_on_scalar(2, 0)
+        regroup_on_gpsimd(2, 1)
+        regroup_on_scalar(3, 0, 0, 2)
+        regroup_on_gpsimd(3, 1)
+        normalise(0, 4)
+        regroup_on_scalar(3, 0, 1, 2)
+        normalise(1, 5)
+        regroup_on_scalar(4, 0, 0, 2)
+        normalise(2, 6)
+        normalise(3, 7)
+        regroup_on_scalar(4, 0, 1, 2)
+        quantise_half(0, 0)
+        quantise_half(1, 0)
         for a in range(TOKEN_TILES):
-            store(0, [a], project(0, [a]))
-        quantise_weights(chunks - 2)
-        rotated_groups = [(1, [0, 1]), (1, [2, 3]), (2, [0, 1]), (2, [2]), (2, [3])]
-        waiting = []
-        for m, group in rotated_groups:
-            waiting.append((m, group, project(m, group)))
-            if len(waiting) == 1:
-                quantise_weights(chunks - 1)
-            else:
-                m_done, group_done, result = waiting[-2]
-                rotate(group_done, result)
-                store(m_done, group_done, result)
-        m_done, group_done, result = waiting[-1]
-        rotate(group_done, result)
-        store(m_done, group_done, result)
+            quantise_x(a)
+        regroup_on_scalar(5, 0, 0, 2)
+        for a in range(TOKEN_TILES):
+            project_v(a, 0)
+        quantise_half(0, 1)
+        quantise_half(1, 1)
+        project_v(0, 1)
+        project_v(1, 1)
+        quantise_weights(2)
+        quantise_weights(3)
+        regroup_on_vector(4, 1)
+        regroup_on_scalar(5, 0, 1, 2)
+        project_v(2, 1)
+        project_v(3, 1)
+        quantise_weights(4)
+        project_rotated(1, 0)
+        regroup_on_vector(5, 1)
+        project_rotated(1, 1)
+        quantise_weights(5)
+        project_rotated(1, 2)
+        project_rotated(1, 3)
+        for a in range(TOKEN_TILES):
+            project_rotated(2, a, last=(a == TOKEN_TILES - 1))

@@ -131,11 +131,11 @@ def tile_transformerlayershard_pa_kernel(
             )
 
         def regroup_on_scalar(c, half, part=0, parts=1):
-            dst, src = regroup_views(c, half, 4, part, parts)
+            dst, src = regroup_views(c, half, 8, part, parts)
             nc.scalar.copy(out=dst, in_=src)
 
         def regroup_on_vector(c, half):
-            dst, src = regroup_views(c, half, 4)
+            dst, src = regroup_views(c, half, 8)
             nc.vector.tensor_copy(out=dst, in_=src)
 
         def regroup_on_gpsimd(c, half):

@@ -29,6 +29,7 @@ BANK = 512
 PSUM_BANKS = 8
 STATS_WIDTH = 512
 STATS_DIM = 6
+SLICES = D_MODEL // P
 HALF = WIDTH // 2
 HALF_HEAD = HEAD_DIM // 2
 EARLY_CHUNKS = 4
@@ -60,7 +61,7 @@ def tile_transformerlayershard_pa_kernel(
         nc.scalar.dma_start(out=cos_bf[:], in_=rope_cos.rearrange("(p a) i -> p a i", a=TOKEN_TILES))
         nc.scalar.dma_start(out=sin_bf[:], in_=rope_sin.rearrange("(p a) i -> p a i", a=TOKEN_TILES))
 
-        affine_rows = keep.tile([P, 2 * D_MODEL], BF16)
+        affine_rows = keep.tile([P, P], BF16)
         nc.vector.memset(affine_rows[:].bitcast(I32), 0)
 
         w_raw = {}
@@ -77,22 +78,24 @@ def tile_transformerlayershard_pa_kernel(
         x_rows = x.flatten_outer_dims().rearrange("(p a) d -> p a d", a=TOKEN_TILES)
         x_sb = keep.tile([P, TOKEN_TILES, D_MODEL], BF16)
         for a in range(TOKEN_TILES):
-            nc.sync.dma_start(out=x_sb[:, a, :], in_=x_rows[:, a, :])
+            width = STATS_WIDTH if a == 0 else D_MODEL
+            for first in range(0, D_MODEL, width):
+                nc.sync.dma_start(out=x_sb[:, a, first : first + width], in_=x_rows[:, a, first : first + width])
+            if a == 1:
+                nc.sync.dma_start(out=affine_rows[0:SLICES, :], in_=ln_scale.rearrange("(j d) -> j d", d=P))
+                nc.sync.dma_start(out=affine_rows[SLICES : 2 * SLICES, :], in_=ln_offset.rearrange("(j d) -> j d", d=P))
             if a % 2 == 1:
                 load_weights(0, (a // 2) * HALF, HALF)
-            if a == 1:
-                nc.sync.dma_start(out=affine_rows[0:1, 0:D_MODEL], in_=ln_scale.rearrange("(o d) -> o d", o=1))
-                nc.sync.dma_start(out=affine_rows[0:1, D_MODEL : 2 * D_MODEL], in_=ln_offset.rearrange("(o d) -> o d", o=1))
         for c in range(1, chunks):
             load_weights(c, 0, WIDTH)
 
-        ones = keep.tile([P, P], BF16)
-        nc.vector.memset(ones[:], 1.0)
         warm = keep.tile([P, 1], F32)
         nc.vector.memset(warm[:], 1.0)
         nc.scalar.sqrt(warm[:], warm[:])
         identity = keep.tile([P, P], F32)
         make_identity(nc, identity[:])
+        identity_bf = keep.tile([P, P], BF16)
+        nc.vector.tensor_copy(out=identity_bf[:], in_=identity[:])
 
         cos_twice = keep.tile([P, TOKEN_TILES, PAIRS, 2], F32)
         nc.gpsimd.tensor_copy(out=cos_twice[:], in_=cos_bf[:].unsqueeze(3).to_broadcast([P, TOKEN_TILES, PAIRS, 2]))
@@ -102,14 +105,18 @@ def tile_transformerlayershard_pa_kernel(
         )
         nc.gpsimd.tensor_copy(out=signed_sin[:, :, :, 1], in_=sin_bf[:])
 
-        affine_banks = []
-        for first in range(0, 2 * D_MODEL, BANK):
-            affine_banks.append(in_bank(first // BANK, [P, BANK], F32, "affine_%d" % first))
-            nc.tensor.matmul(
-                out=affine_banks[-1][:], lhsT=ones[:], rhs=affine_rows[:, first : first + BANK], start=True, stop=True
-            )
-        gain_banks = affine_banks[0 : D_MODEL // BANK]
-        offset_banks = affine_banks[D_MODEL // BANK :]
+        turned = in_bank(0, [P, P], BF16, "turned")
+        nc.tensor.transpose(out=turned[:], in_=affine_rows[:], identity=identity_bf[:])
+        affine_columns = keep.tile([P, 2 * SLICES], BF16)
+        nc.scalar.copy(out=affine_columns[:], in_=turned[:, 0 : 2 * SLICES])
+        gain = in_bank(1, [P, D_MODEL], BF16, "gain")
+        offset = in_bank(2, [P, D_MODEL], BF16, "offset")
+        for bank, first in ((gain, 0), (offset, SLICES)):
+            for j in range(SLICES):
+                nc.tensor.transpose(
+                    out=bank[:, j * P : (j + 1) * P],
+                    in_=affine_columns[:, first + j : first + j + 1].to_broadcast([P, P]), identity=identity_bf[:],
+                )
 
         w_codes = keep.tile([P, chunks, WIDTH], U32, align_bytes=64)
         w_scales = keep.tile([P, chunks, WIDTH], U8, align_bytes=64)
@@ -166,19 +173,20 @@ def tile_transformerlayershard_pa_kernel(
         for a in range(TOKEN_TILES):
             nc.vector.bn_aggr(out=mean_var[:, a, :], in_=stats[:, a, :, :].rearrange("p s v -> p (s v)"))
         rstd = keep.tile([P, TOKEN_TILES], F32)
-        nc.vector.tensor_scalar(out=rstd[:], in0=mean_var[:, :, 1], scalar1=EPS, scalar2=None, op0=ALU.add)
-        nc.scalar.sqrt(rstd[:], rstd[:])
 
         centred = []
         for a in range(TOKEN_TILES):
+            if a == TOKEN_TILES - 1:
+                nc.vector.reciprocal(rstd[:], rstd[:])
             centred.append(per_tile.tile([P, D_MODEL], F32, name="centred"))
-            for h, first in enumerate(range(0, D_MODEL, BANK)):
-                cols = slice(first, first + BANK)
-                nc.vector.scalar_tensor_tensor(
-                    out=centred[a][:, cols], in0=x_sb[:, a, cols], scalar=mean_var[:, a, 0:1],
-                    in1=gain_banks[h][:], op0=ALU.subtract, op1=ALU.mult,
-                )
-        nc.vector.reciprocal(rstd[:], rstd[:])
+            nc.vector.scalar_tensor_tensor(
+                out=centred[a][:], in0=x_sb[:, a, :], scalar=mean_var[:, a, 0:1],
+                in1=gain[:], op0=ALU.subtract, op1=ALU.mult,
+            )
+            if a == 0:
+                nc.vector.tensor_scalar(out=rstd[:], in0=mean_var[:, :, 1], scalar1=EPS, scalar2=None, op0=ALU.add)
+                regroup_on_scalar(1, 0, 0, 2)
+                nc.scalar.sqrt(rstd[:], rstd[:])
 
         x_grouped = {}
         x_codes = keep.tile([P, TOKEN_TILES, PASSES * P], U32, align_bytes=64)
@@ -186,12 +194,9 @@ def tile_transformerlayershard_pa_kernel(
 
         def normalise(a, number):
             xn = per_tile.tile([P, D_MODEL], BF16)
-            for h, first in enumerate(range(0, D_MODEL, BANK)):
-                cols = slice(first, first + BANK)
-                nc.vector.scalar_tensor_tensor(
-                    out=xn[:, cols], in0=centred[a][:, cols], scalar=rstd[:, a : a + 1],
-                    in1=offset_banks[h][:], op0=ALU.mult, op1=ALU.add,
-                )
+            nc.vector.scalar_tensor_tensor(
+                out=xn[:], in0=centred[a][:], scalar=rstd[:, a : a + 1], in1=offset[:], op0=ALU.mult, op1=ALU.add,
+            )
             xn_words = xn[:].bitcast(F32)
             xt = in_bank(number, [P, PASSES * 2, P], F32, "xt")
             for b in range(PASSES * 2):
@@ -250,14 +255,21 @@ def tile_transformerlayershard_pa_kernel(
                 op=ALU.mult,
             )
             nc.scalar.copy(out=r[:, :, HALF_HEAD:], in_=rest[:].rearrange("p (h d) -> p h d", d=HALF_HEAD))
+            rows = output_rows(m, a)
+            if last:
+                rows = rows.rearrange("p (h d) -> p h d", d=HEAD_DIM)
+                nc.sync.dma_start(out=rows[:, :, HALF_HEAD:], in_=r[:, :, HALF_HEAD:])
             nc.scalar.copy(out=r[:, :, ROTATED:HALF_HEAD], in_=u[:, :, ROTATED:])
             adder = nc.vector if last else nc.gpsimd
             adder.tensor_tensor(
                 out=r[:, :, 0:ROTATED], in0=r[:, :, 0:ROTATED], in1=cross[:].rearrange("p h i e -> p h (i e)"), op=ALU.add
             )
-            nc.sync.dma_start(out=output_rows(m, a), in_=result[:])
+            if last:
+                nc.sync.dma_start(out=rows[:, :, 0:HALF_HEAD], in_=r[:, :, 0:HALF_HEAD])
+            else:
+                nc.sync.dma_start(out=rows, in_=result[:])
 
-        regroup_on_scalar(1, 0)
+        regroup_on_scalar(1, 0, 1, 2)
         regroup_on_gpsimd(1, 1)
         regroup_on_scalar(2, 0)
         regroup_on_gpsimd(2, 1)
@@ -282,8 +294,8 @@ def tile_transformerlayershard_pa_kernel(
         project_v(0, 1)
         project_v(1, 1)
         quantise_weights(2)
-        quantise_weights(3)
         regroup_on_vector(4, 1)
+        quantise_weights(3)
         regroup_on_scalar(5, 0, 1, 2)
         project_v(2, 1)
         project_v(3, 1)

from contextlib import ExitStack

import concourse.mybir as mybir
from concourse.masks import make_identity

F32 = mybir.dt.float32
BF16 = mybir.dt.bfloat16
I32 = mybir.dt.int32
U32 = mybir.dt.uint32
U8 = mybir.dt.uint8
FP8X4 = mybir.dt.float8_e4m3fn_x4
ALU = mybir.AluOpType

P = 128
TOKENS = 512
D_MODEL = 1024
HEADS = 4
HEAD_DIM = 256
ROTATED = 64
PAIRS = ROTATED // 2
WIDTH = HEADS * HEAD_DIM
EPS = 1e-5

TOKEN_TILES = TOKENS // P
PACK = 4
K_PASS = P * PACK
PASSES = D_MODEL // K_PASS
BANK = 512
PSUM_BANKS = 8
STATS_WIDTH = 512
STATS_DIM = 6
SLICES = D_MODEL // P
HALF = WIDTH // 2
HALF_HEAD = HEAD_DIM // 2
EARLY_CHUNKS = 4

FLOPS = 2 * TOKENS * D_MODEL * 3 * WIDTH


def tile_transformerlayershard_pa_kernel(
    tc, x, ln_scale, ln_offset, wq, wk, wv, rope_cos, rope_sin, out_0, out_1, out_2
):
    nc = tc.nc
    weights = [wv, wq, wk]
    outputs = [out_2, out_0, out_1]
    chunks = len(weights) * PASSES

    with ExitStack() as stack:
        keep = stack.enter_context(tc.tile_pool(name="keep", bufs=1))
        per_tile = stack.enter_context(tc.tile_pool(name="per_tile", bufs=TOKEN_TILES))
        halves = stack.enter_context(tc.tile_pool(name="halves", bufs=2 * TOKEN_TILES))
        results = stack.enter_context(tc.tile_pool(name="results", bufs=2 * TOKEN_TILES))
        banks = stack.enter_context(tc.psum_pool(name="banks", bufs=1))
        stack.enter_context(tc.manual_schedule())

        def in_bank(number, shape, dtype, name):
            return banks.tile(shape, dtype, name=name, tag="bank_%d" % number)

        cos_bf = keep.tile([P, TOKEN_TILES, PAIRS], BF16)
        sin_bf = keep.tile([P, TOKEN_TILES, PAIRS], BF16)
        nc.scalar.dma_start(out=cos_bf[:], in_=rope_cos.rearrange("(p a) i -> p a i", a=TOKEN_TILES))
        nc.scalar.dma_start(out=sin_bf[:], in_=rope_sin.rearrange("(p a) i -> p a i", a=TOKEN_TILES))

        affine_rows = keep.tile([P, P], BF16)
        nc.vector.memset(affine_rows[:].bitcast(I32), 0)

        w_raw = {}
        w_whole = {}

        def load_weights(c, first, width):
            rows = weights[c // PASSES][(c % PASSES) * K_PASS : (c % PASSES + 1) * K_PASS, first : first + width]
            raw = keep.tile([P, PACK, width], BF16, name="w_raw_%d_%d" % (c, first))
            nc.sync.dma_start(out=raw[:], in_=rows.rearrange("(q t) n -> q t n", t=PACK))
            w_whole[c] = raw[:]
            for half in range(first // HALF, (first + width) // HALF):
                w_raw[c, half] = raw[:, :, half * HALF - first : (half + 1) * HALF - first]

        x_rows = x.flatten_outer_dims().rearrange("(p a) d -> p a d", a=TOKEN_TILES)
        x_sb = keep.tile([P, TOKEN_TILES, D_MODEL], BF16)
        for a in range(TOKEN_TILES):
            width = STATS_WIDTH if a == 0 else D_MODEL
            for first in range(0, D_MODEL, width):
                nc.sync.dma_start(out=x_sb[:, a, first : first + width], in_=x_rows[:, a, first : first + width])
            if a == 1:
                nc.sync.dma_start(out=affine_rows[0:SLICES, :], in_=ln_scale.rearrange("(j d) -> j d", d=P))
                nc.sync.dma_start(out=affine_rows[SLICES : 2 * SLICES, :], in_=ln_offset.rearrange("(j d) -> j d", d=P))
            if a % 2 == 1:
                load_weights(0, (a // 2) * HALF, HALF)
        for c in range(1, chunks):
            load_weights(c, 0, WIDTH)

        warm = keep.tile([P, 1], F32)
        nc.vector.memset(warm[:], 1.0)
        nc.scalar.sqrt(warm[:], warm[:])
        identity = keep.tile([P, P], F32)
        make_identity(nc, identity[:])
        identity_bf = keep.tile([P, P], BF16)
        nc.vector.tensor_copy(out=identity_bf[:], in_=identity[:])

        cos_twice = keep.tile([P, TOKEN_TILES, PAIRS, 2], F32)
        nc.gpsimd.tensor_copy(out=cos_twice[:], in_=cos_bf[:].unsqueeze(3).to_broadcast([P, TOKEN_TILES, PAIRS, 2]))
        signed_sin = keep.tile([P, TOKEN_TILES, PAIRS, 2], F32)
        nc.gpsimd.tensor_scalar(
            out=signed_sin[:, :, :, 0], in0=sin_bf[:], scalar1=-1.0, scalar2=0.0, op0=ALU.mult, op1=ALU.add
        )
        nc.gpsimd.tensor_copy(out=signed_sin[:, :, :, 1], in_=sin_bf[:])

        turned = in_bank(0, [P, P], BF16, "turned")
        nc.tensor.transpose(out=turned[:], in_=affine_rows[:], identity=identity_bf[:])
        affine_columns = keep.tile([P, 2 * SLICES], BF16)
        nc.scalar.copy(out=affine_columns[:], in_=turned[:, 0 : 2 * SLICES])
        gain = in_bank(1, [P, D_MODEL], BF16, "gain")
        offset = in_bank(2, [P, D_MODEL], BF16, "offset")
        for bank, first in ((gain, 0), (offset, SLICES)):
            for j in range(SLICES):
                nc.tensor.transpose(
                    out=bank[:, j * P : (j + 1) * P],
                    in_=affine_columns[:, first + j : first + j + 1].to_broadcast([P, P]), identity=identity_bf[:],
                )

        w_codes = keep.tile([P, chunks, WIDTH], U32, align_bytes=64)
        w_scales = keep.tile([P, chunks, WIDTH], U8, align_bytes=64)
        grouped = []
        for c in range(chunks):
            grouped.append(keep.tile([P, WIDTH, PACK], BF16, name="grouped_%d" % c, align_bytes=64))

        def regroup_views(c, half, run, part=0, parts=1):
            width = HALF // parts
            dst = grouped[c][:, half * HALF + part * width : half * HALF + (part + 1) * width, :]
            if c < PASSES:
                src = w_raw[c, half][:, :, part * width : (part + 1) * width]
                return dst.rearrange("q (n i) t -> q n t i", i=run), src.rearrange("q t (n i) -> q n t i", i=run)
            heads = HEADS // parts
            src = w_whole[c].rearrange("q t (h s d) -> q t s h d", s=2, d=HALF_HEAD)[:, :, half, :, :]
            return (
                dst.rearrange("q (h n i) t -> q h n t i", h=heads, i=run),
                src[:, :, part * heads : (part + 1) * heads, :].rearrange("q t h (n i) -> q h n t i", i=run),
            )

        def regroup_on_scalar(c, half, part=0, parts=1):
            dst, src = regroup_views(c, half, 8, part, parts)
            nc.scalar.copy(out=dst, in_=src)

        def regroup_on_vector(c, half):
            dst, src = regroup_views(c, half, 8)
            nc.vector.tensor_copy(out=dst, in_=src)

        def regroup_on_gpsimd(c, half):
            dst, src = regroup_views(c, half, 1)
            nc.gpsimd.tensor_scalar(out=dst, in0=src, scalar1=1.0, scalar2=0.0, op0=ALU.mult, op1=ALU.add)

        def quantise_half(c, half):
            cols = slice(half * HALF, (half + 1) * HALF)
            nc.vector.quantize_mx(
                out=w_codes[:, c, cols].bitcast(FP8X4), scales=w_scales[:, c, cols],
                in_=grouped[c][:, cols, :].rearrange("q n t -> q (n t)"),
            )

        def quantise_weights(c):
            nc.vector.quantize_mx(
                out=w_codes[:, c, :].bitcast(FP8X4), scales=w_scales[:, c, :],
                in_=grouped[c][:].rearrange("q n t -> q (n t)"),
            )

        regroup_on_scalar(0, 0)
        regroup_on_gpsimd(0, 1)

        stats = keep.tile([P, TOKEN_TILES, D_MODEL // STATS_WIDTH, STATS_DIM], F32)
        mean_var = keep.tile([P, TOKEN_TILES, 2], F32)
        for a in range(TOKEN_TILES):
            for s in range(D_MODEL // STATS_WIDTH):
                nc.vector.bn_stats(out=stats[:, a, s, :], in_=x_sb[:, a, s * STATS_WIDTH : (s + 1) * STATS_WIDTH])
        for a in range(TOKEN_TILES):
            nc.vector.bn_aggr(out=mean_var[:, a, :], in_=stats[:, a, :, :].rearrange("p s v -> p (s v)"))
        rstd = keep.tile([P, TOKEN_TILES], F32)

        centred = []
        for a in range(TOKEN_TILES):
            if a == TOKEN_TILES - 1:
                nc.vector.reciprocal(rstd[:], rstd[:])
            centred.append(per_tile.tile([P, D_MODEL], F32, name="centred"))
            nc.vector.scalar_tensor_tensor(
                out=centred[a][:], in0=x_sb[:, a, :], scalar=mean_var[:, a, 0:1],
                in1=gain[:], op0=ALU.subtract, op1=ALU.mult,
            )
            if a == 0:
                nc.vector.tensor_scalar(out=rstd[:], in0=mean_var[:, :, 1], scalar1=EPS, scalar2=None, op0=ALU.add)
                regroup_on_scalar(1, 0, 0, 2)
                nc.scalar.sqrt(rstd[:], rstd[:])

        x_grouped = {}
        x_codes = keep.tile([P, TOKEN_TILES, PASSES * P], U32, align_bytes=64)
        x_scales = keep.tile([P, TOKEN_TILES, PASSES * P], U8, align_bytes=64)

        def normalise(a, number):
            xn = per_tile.tile([P, D_MODEL], BF16)
            nc.vector.scalar_tensor_tensor(
                out=xn[:], in0=centred[a][:], scalar=rstd[:, a : a + 1], in1=offset[:], op0=ALU.mult, op1=ALU.add,
            )
            xn_words = xn[:].bitcast(F32)
            xt = in_bank(number, [P, PASSES * 2, P], F32, "xt")
            for b in range(PASSES * 2):
                nc.tensor.transpose(
                    out=xt[:, b, :], in_=xn_words[:, (b // 2) * 2 * P + b % 2 : (b // 2 + 1) * 2 * P : 2], identity=identity[:]
                )
            x_grouped[a] = per_tile.tile([P, PASSES * P * PACK], BF16, name="x_grouped", align_bytes=64)
            nc.scalar.copy(
                out=x_grouped[a][:].bitcast(F32).rearrange("q (g r u) -> q g r u", g=PASSES, u=2),
                in_=xt[:].rearrange("q (g u) r -> q g r u", u=2),
            )

        def quantise_x(a):
            nc.vector.quantize_mx(out=x_codes[:, a, :].bitcast(FP8X4), scales=x_scales[:, a, :], in_=x_grouped[a][:])

        bank_order = [4, 5, 6, 7, 0, 1, 2, 3]
        taken = []

        def multiply(m, a, first):
            bank = in_bank(bank_order[len(taken) % PSUM_BANKS], [P, BANK], F32, "product")
            taken.append(bank)
            for g in range(PASSES):
                nc.tensor.matmul_mx(
                    out=bank[:],
                    lhsT=x_codes[:, a, g * P : (g + 1) * P].bitcast(FP8X4),
                    lhsT_scale=x_scales[:, a, g * P : (g + 1) * P],
                    rhs=w_codes[:, m * PASSES + g, first : first + BANK].bitcast(FP8X4),
                    rhs_scale=w_scales[:, m * PASSES + g, first : first + BANK],
                    start=(g == 0),
                    stop=(g == PASSES - 1),
                )
            return bank

        def output_rows(m, a):
            return outputs[m].flatten_outer_dims().rearrange("(p a h) d -> p a (h d)", a=TOKEN_TILES, h=HEADS)[:, a, :]

        def project_v(a, half):
            cols = slice(half * HALF, (half + 1) * HALF)
            result = halves.tile([P, HALF], F32, name="value")
            nc.scalar.copy(out=result[:], in_=multiply(0, a, half * HALF)[:])
            nc.sync.dma_start(out=output_rows(0, a)[:, cols], in_=result[:])

        def project_rotated(m, a, last=False):
            result = results.tile([P, WIDTH], F32, name="result")
            u = multiply(m, a, 0)[:].rearrange("p (h d) -> p h d", d=HALF_HEAD)
            rest = multiply(m, a, BANK)
            r = result[:].rearrange("p (h d) -> p h d", d=HEAD_DIM)
            cross = per_tile.tile([P, HEADS, PAIRS, 2], F32, name="cross")
            nc.vector.tensor_tensor(
                out=cross[:], in0=u[:, :, 0:ROTATED].rearrange("p h (i e) -> p h i e", e=2)[:, :, :, ::-1],
                in1=signed_sin[:, a, :, :].unsqueeze(1).to_broadcast([P, HEADS, PAIRS, 2]), op=ALU.mult,
            )
            nc.vector.tensor_tensor(
                out=r[:, :, 0:ROTATED], in0=u[:, :, 0:ROTATED],
                in1=cos_twice[:, a, :, :].rearrange("p i e -> p (i e)").unsqueeze(1).to_broadcast([P, HEADS, ROTATED]),
                op=ALU.mult,
            )
            nc.scalar.copy(out=r[:, :, HALF_HEAD:], in_=rest[:].rearrange("p (h d) -> p h d", d=HALF_HEAD))
            rows = output_rows(m, a)
            if last:
                rows = rows.rearrange("p (h d) -> p h d", d=HEAD_DIM)
                nc.sync.dma_start(out=rows[:, :, HALF_HEAD:], in_=r[:, :, HALF_HEAD:])
            nc.scalar.copy(out=r[:, :, ROTATED:HALF_HEAD], in_=u[:, :, ROTATED:])
            adder = nc.vector if last else nc.gpsimd
            adder.tensor_tensor(
                out=r[:, :, 0:ROTATED], in0=r[:, :, 0:ROTATED], in1=cross[:].rearrange("p h i e -> p h (i e)"), op=ALU.add
            )
            if last:
                nc.sync.dma_start(out=rows[:, :, 0:HALF_HEAD], in_=r[:, :, 0:HALF_HEAD])
            else:
                nc.sync.dma_start(out=rows, in_=result[:])

        regroup_on_scalar(1, 0, 1, 2)
        regroup_on_gpsimd(1, 1)
        regroup_on_scalar(2, 0)
        regroup_on_gpsimd(2, 1)
        regroup_on_scalar(3, 0, 0, 2)
        regroup_on_gpsimd(3, 1)
        normalise(0, 4)
        regroup_on_scalar(3, 0, 1, 2)
        normalise(1, 5)
        regroup_on_scalar(4, 0, 0, 2)
        normalise(2, 6)
        normalise(3, 7)
        regroup_on_scalar(4, 0, 1, 2)
        quantise_half(0, 0)
        quantise_half(1, 0)
        for a in range(TOKEN_TILES):
            quantise_x(a)
        regroup_on_scalar(5, 0, 0, 2)
        for a in range(TOKEN_TILES):
            project_v(a, 0)
        quantise_half(0, 1)
        quantise_half(1, 1)
        project_v(0, 1)
        project_v(1, 1)
        quantise_weights(2)
        regroup_on_vector(4, 1)
        quantise_weights(3)
        regroup_on_scalar(5, 0, 1, 2)
        project_v(2, 1)
        project_v(3, 1)
        quantise_weights(4)
        project_rotated(1, 0)
        regroup_on_vector(5, 1)
        project_rotated(1, 1)
        quantise_weights(5)
        project_rotated(1, 2)
        project_rotated(1, 3)
        for a in range(TOKEN_TILES):
            project_rotated(2, a, last=(a == TOKEN_TILES - 1))
